import numpy as np
import ml_dtypes


def mxq(x, axis, fmt="e4m3"):
    dtype, down = {"e4m3": (ml_dtypes.float8_e4m3fn, 7), "e5m2": (ml_dtypes.float8_e5m2, 14)}[fmt]
    v = np.moveaxis(np.asarray(x, np.float32).astype(ml_dtypes.bfloat16).astype(np.float64), axis, -1)
    blocks = v.reshape(v.shape[:-1] + (-1, 32))
    amax = np.abs(blocks).max(-1, keepdims=True)
    byte = np.maximum(np.where(amax > 0, np.frexp(amax)[1] - 1 + 127, 0) - down, 1)
    scale = np.exp2(byte - 127.0)
    codes = (blocks / scale).astype(np.float32).astype(dtype).astype(np.float64)
    return np.moveaxis((codes * scale).reshape(v.shape), -1, axis)


WIDE = False


def mx_kscale(k):
    if not WIDE:
        return np.ones(k)
    levels = np.array([10, -10, 5, -5, 0])
    a = np.random.permutation(np.resize(levels, k // 512 * 4)).reshape(k // 512, 4)
    idx = np.arange(k)
    return np.exp2(a[idx // 512, idx % 128 // 32])


BF16 = ml_dtypes.bfloat16


def bf(x):
    return np.asarray(x, np.float32).astype(BF16)


def f64(x):
    return np.asarray(x).astype(np.float64)


B, K, NH, N = 512, 2048, 4096, 1024
EPSILON = 0.1


def setup_inputs():
    s = mx_kscale(K)
    g = 1.0 / np.mean(1.0 / s)
    return {"x": bf(np.random.standard_normal((B, K)) * s),
            "y": bf(np.random.standard_normal((B, N)) * 12.0 / np.sqrt(K) * g),
            "beta": bf(np.random.random((K, N)) * 1.7 / np.sqrt(K) / s[:, None]),
            "bias_lin": bf(np.random.standard_normal(N) * 0.1),
            "W1": bf(-np.random.random((NH, K)) * 1.7 / np.sqrt(K) / s[None, :]),
            "W2": bf(np.random.random((N, NH)) * (0.5 + np.random.random((N, 1))) * 2.0 / NH**2),
            "bias1": bf(np.random.standard_normal(NH) * 0.1),
            "bias2": bf(np.random.standard_normal(N) * 0.1),
            "adv": 1}


def reference(x, y, beta, bias_lin, W1, W2, bias1, bias2, adv):
    xq = mxq(f64(x), 1, "e4m3")
    lin = (xq @ mxq(f64(beta), 0, "e4m3")) + f64(bias_lin)
    if adv:
        beta_norm = np.sum(np.abs(f64(beta)), axis=0)
        lin = lin - EPSILON * f64(y) * beta_norm
    if adv:
        one = NH * np.sum(f64(W2), axis=1) + f64(bias2)
        one = np.broadcast_to(one, lin.shape)
    else:
        h = np.maximum((xq @ mxq(f64(W1), 1, "e4m3").T) + f64(bias1), 0.0)
        one = (mxq(h, 1, "e4m3") @ mxq(f64(W2), 1, "e4m3").T) + f64(bias2)
    return lin + one

@@ -1,0 +1,227 @@
+from contextlib import ExitStack
+
+import concourse.mybir as mybir
+from concourse.masks import make_identity
+
+F32 = mybir.dt.float32
+BF16 = mybir.dt.bfloat16
+I32 = mybir.dt.int32
+U32 = mybir.dt.uint32
+U8 = mybir.dt.uint8
+FP8X4 = mybir.dt.float8_e4m3fn_x4
+ALU = mybir.AluOpType
+ACT = mybir.ActivationFunctionType
+
+P = 128
+B, K, NH, N = 512, 2048, 4096, 1024
+EPSILON = 0.1
+PASSES = K // 512
+JT = N // P
+BT = B // P
+ONES_N = 32
+
+FLOPS = 2 * B * K * N
+BYTES = 2 * (B * K + B * N + K * N + N * NH + 2 * N) + 4 * B * N
+
+SCALAR_TILES = (2, 5)
+
+
+def tile_advresnet_kernel(tc, x, y, beta, bias_lin, W1, W2, bias1, bias2, adv, out):
+    assert adv == 1
+    nc = tc.nc
+    with ExitStack() as ctx:
+        const = ctx.enter_context(tc.tile_pool(name="const", bufs=1))
+        big = ctx.enter_context(tc.tile_pool(name="big", bufs=1))
+        work = ctx.enter_context(tc.tile_pool(name="work", bufs=2))
+        ps_a = ctx.enter_context(tc.psum_pool(name="ps_a", bufs=4))
+        ps_b = ctx.enter_context(tc.psum_pool(name="ps_b", bufs=2))
+        ps_c = ctx.enter_context(tc.psum_pool(name="ps_c", bufs=2))
+
+        brows = const.tile([P, P], BF16, name="brows")
+        nc.gpsimd.memset(brows[:], 0.0)
+        nc.scalar.dma_start(out=brows[0:8, :], in_=bias_lin.rearrange("(r c) -> r c", c=P))
+        nc.scalar.dma_start(out=brows[8:16, :], in_=bias2.rearrange("(r c) -> r c", c=P))
+        ident_b = const.tile([P, P], BF16, name="ident_b")
+        make_identity(nc, ident_b[:])
+        ident_f = const.tile([P, P], F32, name="ident_f")
+        make_identity(nc, ident_f[:])
+        ones = const.tile([P, ONES_N], BF16, name="ones")
+        nc.vector.memset(ones[:], 1.0)
+
+        raw = big.tile([P, PASSES * 4096], BF16, name="raw", tag="raw_tt")
+        for g in range(PASSES):
+            nc.sync.dma_start(
+                out=raw[:, 4096 * g : 4096 * (g + 1)].rearrange("q (u r) -> q u r", u=2),
+                in_=beta[512 * g : 512 * (g + 1), :].rearrange("(u q e) w -> q u (e w)", u=2, e=2),
+            )
+        x_sb = big.tile([P, BT * K], BF16, name="x_sb", tag="x_out")
+        x_rows = x.rearrange("(p t) k -> p (t k)", t=BT)
+        for h in range(2):
+            nc.sync.dma_start(out=x_sb[:, 4096 * h : 4096 * (h + 1)], in_=x_rows[:, 4096 * h : 4096 * (h + 1)])
+        y_sb = big.tile([P, BT * N], BF16, name="y_sb")
+        nc.sync.dma_start(out=y_sb[:], in_=y.rearrange("(p t) j -> p (t j)", t=BT))
+        w2 = [big.tile([P, NH], BF16, name="w2_%d" % jt) for jt in range(JT)]
+        for jt in range(JT - 1):
+            nc.sync.dma_start(out=w2[jt][:], in_=W2[P * jt : P * (jt + 1), :])
+        for i in range(2):
+            nc.sync.dma_start(
+                out=w2[JT - 1][:, 2048 * i : 2048 * (i + 1)],
+                in_=W2[P * (JT - 1) : P * JT, 2048 * i : 2048 * (i + 1)],
+            )
+
+        bt_ps = ps_c.tile([P, P], BF16, name="bt_ps", tag="c")
+        nc.tensor.transpose(out=bt_ps[:], in_=brows[:], identity=ident_b[:])
+        b16 = const.tile([P, 16], F32, name="b16")
+        nc.vector.tensor_copy(out=b16[:], in_=bt_ps[:, 0:16])
+        bsum = const.tile([P, JT], F32, name="bsum")
+        nc.vector.tensor_tensor(out=bsum[:], in0=b16[:, 0:8], in1=b16[:, 8:16], op=ALU.add)
+
+        codes_b = big.tile([P, PASSES * N], U32, name="codes_b", align_bytes=64)
+        plane_b = big.tile([P, PASSES * N], U8, name="plane_b", align_bytes=64)
+        bn = [ps_b.tile([P, 4, PASSES, ONES_N], F32, name="bn_%d" % i, tag="b") for i in range(2)]
+        for g in range(PASSES):
+            pas = raw[:, 4096 * g : 4096 * (g + 1)]
+            ab = work.tile([P, 2048], I32, name="ab", tag="ab")
+            nc.vector.tensor_single_scalar(out=ab[:], in_=pas.bitcast(I32), scalar=0x7FFF7FFF, op=ALU.bitwise_and)
+            planes = pas.rearrange("q (t w) -> q t w", t=4)
+            gbs = []
+            for h in range(2):
+                gb = work.tile([P, 2048], BF16, name="gb", tag="gb", bufs=4, align_bytes=64)
+                src = planes[:, :, 512 * h : 512 * (h + 1)].rearrange("q t (c i) -> q c t i", i=4)
+                dst = gb[:].rearrange("q (c i t) -> q c t i", i=4, t=4)
+                if h == 0:
+                    nc.vector.tensor_copy(out=dst, in_=src)
+                else:
+                    nc.scalar.copy(out=dst, in_=src)
+                gbs.append(gb)
+            for h in range(2):
+                cols = slice(N * g + 512 * h, N * g + 512 * (h + 1))
+                nc.vector.quantize_mx(out=codes_b[:, cols].bitcast(FP8X4), scales=plane_b[:, cols], in_=gbs[h][:])
+            abv = ab[:].bitcast(BF16)
+            for jt in range(JT):
+                for t in range(4):
+                    nc.tensor.matmul(
+                        out=bn[jt // 4][:, jt % 4, g, :],
+                        lhsT=abv[:, N * t + P * jt : N * t + P * (jt + 1)],
+                        rhs=ones[:],
+                        start=(t == 0),
+                        stop=(t == 3),
+                    )
+        sraw = const.tile([P, JT], F32, name="sraw")
+        for i in range(2):
+            nc.vector.tensor_reduce(
+                out=sraw[:, 4 * i : 4 * (i + 1)], in_=bn[i][:, :, :, 0], axis=mybir.AxisListType.X, op=ALU.add
+            )
+        s_col = const.tile([P, JT], F32, name="s_col")
+        nc.vector.tensor_scalar_mul(out=s_col[:], in0=sraw[:], scalar1=-EPSILON)
+
+        codes_x = big.tile([P, PASSES * B], U32, name="codes_x", align_bytes=64)
+        plane_x = big.tile([P, PASSES * B], U8, name="plane_x", align_bytes=64)
+        xw = x_sb[:].bitcast(F32)
+        for h in range(2):
+            for g in range(PASSES):
+                xt = ps_a.tile([P, 2, 256], F32, name="xt", tag="a")
+                for u in range(2):
+                    for tt in range(2):
+                        w0 = 1024 * (2 * h + tt) + 256 * g + 128 * u
+                        nc.tensor.transpose(
+                            out=xt[:, u, P * tt : P * (tt + 1)], in_=xw[:, w0 : w0 + P], identity=ident_f[:]
+                        )
+                gx = work.tile([P, 1024], BF16, name="gx", tag="gx", bufs=3, align_bytes=64)
+                nc.scalar.copy(
+                    out=gx[:].bitcast(F32).rearrange("q (c u) -> q c u", u=2), in_=xt[:].rearrange("q u c -> q c u")
+                )
+                cols = slice(B * g + 256 * h, B * g + 256 * (h + 1))
+                nc.vector.quantize_mx(out=codes_x[:, cols].bitcast(FP8X4), scales=plane_x[:, cols], in_=gx[:])
+
+        t_all = big.tile([P, JT, B], F32, name="t_all", tag="raw_tt")
+        for jt in range(JT):
+            y_t = ps_c.tile([P, B], BF16, name="y_t", tag="c")
+            for t in range(BT):
+                nc.tensor.transpose(
+                    out=y_t[:, P * t : P * (t + 1)],
+                    in_=y_sb[:, N * t + P * jt : N * t + P * (jt + 1)],
+                    identity=ident_b[:],
+                )
+            nc.scalar.activation(
+                out=t_all[:, jt, :],
+                in_=y_t[:],
+                func=ACT.Identity,
+                scale=s_col[:, jt : jt + 1],
+                bias=bsum[:, jt : jt + 1],
+            )
+
+        out_sb = big.tile([P, BT, N], F32, name="out_sb", tag="x_out")
+        out_v = out.rearrange("(p t) j -> p t j", t=BT)
+        for jt in range(JT):
+            c_col = const.tile([P, 1], F32, name="c_%d" % jt)
+            if jt in SCALAR_TILES:
+                part = const.tile([P, 2], F32, name="part_%d" % jt)
+                for i in range(2):
+                    piece = w2[jt][:, 2048 * i : 2048 * (i + 1)]
+                    nc.scalar.activation(
+                        out=piece, in_=piece, func=ACT.Copy, scale=float(NH), accum_out=part[:, i : i + 1]
+                    )
+                nc.vector.tensor_tensor(out=c_col[:], in0=part[:, 0:1], in1=part[:, 1:2], op=ALU.add)
+            elif jt == JT - 1:
+                pa = const.tile([P, 1], F32, name="pa")
+                pb = const.tile([P, 1], F32, name="pb")
+                junk = work.tile([P, 1024], F32, name="junk", tag="junk", bufs=1)
+                nc.vector.scalar_tensor_tensor(
+                    out=junk[:],
+                    in0=w2[jt][:, 0:1024],
+                    scalar=1.0,
+                    in1=w2[jt][:, 1024:2048],
+                    op0=ALU.mult,
+                    op1=ALU.add,
+                    accum_out=pa[:],
+                )
+                nc.vector.tensor_scalar(
+                    out=w2[jt][:, 2048:4096],
+                    in0=w2[jt][:, 2048:4096],
+                    scalar1=float(NH),
+                    scalar2=None,
+                    op0=ALU.mult,
+                    op1=ALU.add,
+                    accum_out=pb[:],
+                )
+                nc.vector.scalar_tensor_tensor(
+                    out=c_col[:], in0=pa[:], scalar=float(NH), in1=pb[:], op0=ALU.mult, op1=ALU.add
+                )
+            else:
+                nc.vector.tensor_scalar(
+                    out=w2[jt][:],
+                    in0=w2[jt][:],
+                    scalar1=float(NH),
+                    scalar2=None,
+                    op0=ALU.mult,
+                    op1=ALU.add,
+                    accum_out=c_col[:],
+                )
+            mm = ps_a.tile([P, B], F32, name="mm", tag="a")
+            for g in range(PASSES):
+                jc = slice(N * g + P * jt, N * g + P * (jt + 1))
+                bc = slice(B * g, B * (g + 1))
+                nc.tensor.matmul_mx(
+                    out=mm[:],
+                    lhsT=codes_b[:, jc].bitcast(FP8X4),
+                    lhsT_scale=plane_b[:, jc],
+                    rhs=codes_x[:, bc].bitcast(FP8X4),
+                    rhs_scale=plane_x[:, bc],
+                    start=(g == 0),
+                    stop=(g == PASSES - 1),
+                )
+            o_t = work.tile([P, B], F32, name="o_t", tag="o_t", bufs=3)
+            nc.vector.scalar_tensor_tensor(
+                out=o_t[:], in0=mm[:], scalar=c_col[:, 0:1], in1=t_all[:, jt, :], op0=ALU.add, op1=ALU.add
+            )
+            o_ps = ps_b.tile([P, BT, P], F32, name="o_ps", tag="b")
+            for t in range(BT):
+                nc.tensor.transpose(out=o_ps[:, t, :], in_=o_t[:, P * t : P * (t + 1)], identity=ident_f[:])
+            nc.scalar.copy(out=out_sb[:, :, P * jt : P * (jt + 1)], in_=o_ps[:])
+            if jt >= 6:
+                sc = slice(P * jt, P * (jt + 1))
+                nc.sync.dma_start(out=out_v[:, :, sc], in_=out_sb[:, :, sc])
+            elif jt % 2 == 1:
+                sc = slice(P * (jt - 1), P * (jt + 1))
+                nc.sync.dma_start(out=out_v[:, :, sc], in_=out_sb[:, :, sc])

@@ -23,7 +23,7 @@ ONES_N = 32
 FLOPS = 2 * B * K * N
 BYTES = 2 * (B * K + B * N + K * N + N * NH + 2 * N) + 4 * B * N
 
-SCALAR_TILES = (2, 5)
+LOAD_ORDER = (0, 1, 3, 2, 6, 4, 5)
 
 
 def tile_advresnet_kernel(tc, x, y, beta, bias_lin, W1, W2, bias1, bias2, adv, out):
@@ -33,9 +33,10 @@ def tile_advresnet_kernel(tc, x, y, beta, bias_lin, W1, W2, bias1, bias2, adv, o
         const = ctx.enter_context(tc.tile_pool(name="const", bufs=1))
         big = ctx.enter_context(tc.tile_pool(name="big", bufs=1))
         work = ctx.enter_context(tc.tile_pool(name="work", bufs=2))
-        ps_a = ctx.enter_context(tc.psum_pool(name="ps_a", bufs=4))
-        ps_b = ctx.enter_context(tc.psum_pool(name="ps_b", bufs=2))
+        ps_a = ctx.enter_context(tc.psum_pool(name="ps_a", bufs=3))
+        ps_b = ctx.enter_context(tc.psum_pool(name="ps_b", bufs=3))
         ps_c = ctx.enter_context(tc.psum_pool(name="ps_c", bufs=2))
+        ctx.enter_context(tc.manual_schedule())
 
         brows = const.tile([P, P], BF16, name="brows")
         nc.gpsimd.memset(brows[:], 0.0)
@@ -49,7 +50,14 @@ def tile_advresnet_kernel(tc, x, y, beta, bias_lin, W1, W2, bias1, bias2, adv, o
         nc.vector.memset(ones[:], 1.0)
 
         raw = big.tile([P, PASSES * 4096], BF16, name="raw", tag="raw_tt")
-        for g in range(PASSES):
+        raw_planes = raw[:].rearrange("q (g t w) -> q g t w", g=PASSES, t=4)
+        for h in range(2):
+            for u in range(2):
+                nc.sync.dma_start(
+                    out=raw_planes[:, 0, 2 * u : 2 * u + 2, 512 * h : 512 * (h + 1)],
+                    in_=beta[256 * u : 256 * (u + 1), 512 * h : 512 * (h + 1)].rearrange("(q e) w -> q e w", e=2),
+                )
+        for g in range(1, PASSES):
             nc.sync.dma_start(
                 out=raw[:, 4096 * g : 4096 * (g + 1)].rearrange("q (u r) -> q u r", u=2),
                 in_=beta[512 * g : 512 * (g + 1), :].rearrange("(u q e) w -> q u (e w)", u=2, e=2),
@@ -61,7 +69,7 @@ def tile_advresnet_kernel(tc, x, y, beta, bias_lin, W1, W2, bias1, bias2, adv, o
         y_sb = big.tile([P, BT * N], BF16, name="y_sb")
         nc.sync.dma_start(out=y_sb[:], in_=y.rearrange("(p t) j -> p (t j)", t=BT))
         w2 = [big.tile([P, NH], BF16, name="w2_%d" % jt) for jt in range(JT)]
-        for jt in range(JT - 1):
+        for jt in LOAD_ORDER:
             nc.sync.dma_start(out=w2[jt][:], in_=W2[P * jt : P * (jt + 1), :])
         for i in range(2):
             nc.sync.dma_start(
@@ -69,35 +77,54 @@ def tile_advresnet_kernel(tc, x, y, beta, bias_lin, W1, W2, bias1, bias2, adv, o
                 in_=W2[P * (JT - 1) : P * JT, 2048 * i : 2048 * (i + 1)],
             )
 
-        bt_ps = ps_c.tile([P, P], BF16, name="bt_ps", tag="c")
-        nc.tensor.transpose(out=bt_ps[:], in_=brows[:], identity=ident_b[:])
-        b16 = const.tile([P, 16], F32, name="b16")
-        nc.vector.tensor_copy(out=b16[:], in_=bt_ps[:, 0:16])
-        bsum = const.tile([P, JT], F32, name="bsum")
-        nc.vector.tensor_tensor(out=bsum[:], in0=b16[:, 0:8], in1=b16[:, 8:16], op=ALU.add)
-
         codes_b = big.tile([P, PASSES * N], U32, name="codes_b", align_bytes=64)
         plane_b = big.tile([P, PASSES * N], U8, name="plane_b", align_bytes=64)
+        codes_x = big.tile([P, PASSES * B], U32, name="codes_x", align_bytes=64)
+        plane_x = big.tile([P, PASSES * B], U8, name="plane_x", align_bytes=64)
+        b16 = const.tile([P, 16], F32, name="b16")
+        bsum = const.tile([P, JT], F32, name="bsum")
+        sraw = const.tile([P, JT], F32, name="sraw")
+        s_col = const.tile([P, JT], F32, name="s_col")
+        c_col = [const.tile([P, 1], F32, name="c_%d" % jt) for jt in range(JT)]
+        part_a = [const.tile([P, 1], F32, name="pa_%d" % jt) for jt in range(JT)]
+        part_b = [const.tile([P, 1], F32, name="pb_%d" % jt) for jt in range(JT)]
+        xw = x_sb[:].bitcast(F32)
+        out_v = out.rearrange("(p t) j -> p t j", t=BT)
+        held = {}
+
+        bt_ps = ps_c.tile([P, P], BF16, name="bt_ps", tag="c")
+        nc.tensor.transpose(out=bt_ps[:], in_=brows[:], identity=ident_b[:])
         bn = [ps_b.tile([P, 4, PASSES, ONES_N], F32, name="bn_%d" % i, tag="b") for i in range(2)]
-        for g in range(PASSES):
-            pas = raw[:, 4096 * g : 4096 * (g + 1)]
+
+        def bias_cols():
+            nc.vector.tensor_copy(out=b16[:], in_=bt_ps[:, 0:16])
+            nc.vector.tensor_tensor(out=bsum[:], in0=b16[:, 0:8], in1=b16[:, 8:16], op=ALU.add)
+
+        def beta_abs(g):
             ab = work.tile([P, 2048], I32, name="ab", tag="ab")
-            nc.vector.tensor_single_scalar(out=ab[:], in_=pas.bitcast(I32), scalar=0x7FFF7FFF, op=ALU.bitwise_and)
-            planes = pas.rearrange("q (t w) -> q t w", t=4)
-            gbs = []
-            for h in range(2):
-                gb = work.tile([P, 2048], BF16, name="gb", tag="gb", bufs=4, align_bytes=64)
-                src = planes[:, :, 512 * h : 512 * (h + 1)].rearrange("q t (c i) -> q c t i", i=4)
-                dst = gb[:].rearrange("q (c i t) -> q c t i", i=4, t=4)
-                if h == 0:
-                    nc.vector.tensor_copy(out=dst, in_=src)
-                else:
-                    nc.scalar.copy(out=dst, in_=src)
-                gbs.append(gb)
-            for h in range(2):
-                cols = slice(N * g + 512 * h, N * g + 512 * (h + 1))
-                nc.vector.quantize_mx(out=codes_b[:, cols].bitcast(FP8X4), scales=plane_b[:, cols], in_=gbs[h][:])
-            abv = ab[:].bitcast(BF16)
+            nc.vector.tensor_single_scalar(
+                out=ab[:], in_=raw[:, 4096 * g : 4096 * (g + 1)].bitcast(I32), scalar=0x7FFF7FFF, op=ALU.bitwise_and
+            )
+            held["ab", g] = ab
+
+        def beta_copy(g, h, on_vector):
+            gb = work.tile([P, 2048], BF16, name="gb", tag="gb", bufs=8, align_bytes=64)
+            src = raw_planes[:, g, :, 512 * h : 512 * (h + 1)].rearrange("q t (c i) -> q c t i", i=4)
+            dst = gb[:].rearrange("q (c i t) -> q c t i", i=4, t=4)
+            if on_vector:
+                nc.vector.tensor_copy(out=dst, in_=src)
+            else:
+                nc.scalar.copy(out=dst, in_=src)
+            held["gb", g, h] = gb
+
+        def beta_quant(g, h):
+            cols = slice(N * g + 512 * h, N * g + 512 * (h + 1))
+            nc.vector.quantize_mx(
+                out=codes_b[:, cols].bitcast(FP8X4), scales=plane_b[:, cols], in_=held["gb", g, h][:]
+            )
+
+        def beta_norm(g):
+            abv = held["ab", g][:].bitcast(BF16)
             for jt in range(JT):
                 for t in range(4):
                     nc.tensor.matmul(
@@ -107,97 +134,56 @@ def tile_advresnet_kernel(tc, x, y, beta, bias_lin, W1, W2, bias1, bias2, adv, o
                         start=(t == 0),
                         stop=(t == 3),
                     )
-        sraw = const.tile([P, JT], F32, name="sraw")
-        for i in range(2):
-            nc.vector.tensor_reduce(
-                out=sraw[:, 4 * i : 4 * (i + 1)], in_=bn[i][:, :, :, 0], axis=mybir.AxisListType.X, op=ALU.add
+
+        def norm_cols():
+            for i in range(2):
+                nc.vector.tensor_reduce(
+                    out=sraw[:, 4 * i : 4 * (i + 1)], in_=bn[i][:, :, :, 0], axis=mybir.AxisListType.X, op=ALU.add
+                )
+            nc.vector.tensor_scalar_mul(out=s_col[:], in0=sraw[:], scalar1=-EPSILON)
+
+        def x_turn(i):
+            h, g = i // PASSES, i % PASSES
+            xt = ps_a.tile([P, 2, 256], F32, name="xt", tag="a")
+            for u in range(2):
+                for tt in range(2):
+                    w0 = 1024 * (2 * h + tt) + 256 * g + 128 * u
+                    nc.tensor.transpose(
+                        out=xt[:, u, P * tt : P * (tt + 1)], in_=xw[:, w0 : w0 + P], identity=ident_f[:]
+                    )
+            gx = work.tile([P, 1024], BF16, name="gx", tag="gx", bufs=8, align_bytes=64)
+            nc.scalar.copy(
+                out=gx[:].bitcast(F32).rearrange("q (c u) -> q c u", u=2), in_=xt[:].rearrange("q u c -> q c u")
             )
-        s_col = const.tile([P, JT], F32, name="s_col")
-        nc.vector.tensor_scalar_mul(out=s_col[:], in0=sraw[:], scalar1=-EPSILON)
+            held["gx", i] = gx
 
-        codes_x = big.tile([P, PASSES * B], U32, name="codes_x", align_bytes=64)
-        plane_x = big.tile([P, PASSES * B], U8, name="plane_x", align_bytes=64)
-        xw = x_sb[:].bitcast(F32)
-        for h in range(2):
-            for g in range(PASSES):
-                xt = ps_a.tile([P, 2, 256], F32, name="xt", tag="a")
-                for u in range(2):
-                    for tt in range(2):
-                        w0 = 1024 * (2 * h + tt) + 256 * g + 128 * u
-                        nc.tensor.transpose(
-                            out=xt[:, u, P * tt : P * (tt + 1)], in_=xw[:, w0 : w0 + P], identity=ident_f[:]
-                        )
-                gx = work.tile([P, 1024], BF16, name="gx", tag="gx", bufs=3, align_bytes=64)
-                nc.scalar.copy(
-                    out=gx[:].bitcast(F32).rearrange("q (c u) -> q c u", u=2), in_=xt[:].rearrange("q u c -> q c u")
-                )
-                cols = slice(B * g + 256 * h, B * g + 256 * (h + 1))
-                nc.vector.quantize_mx(out=codes_x[:, cols].bitcast(FP8X4), scales=plane_x[:, cols], in_=gx[:])
+        def x_quant(i):
+            h, g = i // PASSES, i % PASSES
+            cols = slice(B * g + 256 * h, B * g + 256 * (h + 1))
+            nc.vector.quantize_mx(out=codes_x[:, cols].bitcast(FP8X4), scales=plane_x[:, cols], in_=held["gx", i][:])
 
-        t_all = big.tile([P, JT, B], F32, name="t_all", tag="raw_tt")
-        for jt in range(JT):
-            y_t = ps_c.tile([P, B], BF16, name="y_t", tag="c")
-            for t in range(BT):
-                nc.tensor.transpose(
-                    out=y_t[:, P * t : P * (t + 1)],
-                    in_=y_sb[:, N * t + P * jt : N * t + P * (jt + 1)],
-                    identity=ident_b[:],
-                )
+        def y_turn(m):
+            y_t = ps_c.tile([P, 2, B], BF16, name="y_t", tag="c")
+            for i in range(2):
+                jt = 2 * m + i
+                for t in range(BT):
+                    nc.tensor.transpose(
+                        out=y_t[:, i, P * t : P * (t + 1)],
+                        in_=y_sb[:, N * t + P * jt : N * t + P * (jt + 1)],
+                        identity=ident_b[:],
+                    )
+            held["y_t", m] = y_t
+
+        def y_term(jt):
             nc.scalar.activation(
-                out=t_all[:, jt, :],
-                in_=y_t[:],
+                out=held["t_all"][:, jt, :],
+                in_=held["y_t", jt // 2][:, jt % 2, :],
                 func=ACT.Identity,
                 scale=s_col[:, jt : jt + 1],
                 bias=bsum[:, jt : jt + 1],
             )
 
-        out_sb = big.tile([P, BT, N], F32, name="out_sb", tag="x_out")
-        out_v = out.rearrange("(p t) j -> p t j", t=BT)
-        for jt in range(JT):
-            c_col = const.tile([P, 1], F32, name="c_%d" % jt)
-            if jt in SCALAR_TILES:
-                part = const.tile([P, 2], F32, name="part_%d" % jt)
-                for i in range(2):
-                    piece = w2[jt][:, 2048 * i : 2048 * (i + 1)]
-                    nc.scalar.activation(
-                        out=piece, in_=piece, func=ACT.Copy, scale=float(NH), accum_out=part[:, i : i + 1]
-                    )
-                nc.vector.tensor_tensor(out=c_col[:], in0=part[:, 0:1], in1=part[:, 1:2], op=ALU.add)
-            elif jt == JT - 1:
-                pa = const.tile([P, 1], F32, name="pa")
-                pb = const.tile([P, 1], F32, name="pb")
-                junk = work.tile([P, 1024], F32, name="junk", tag="junk", bufs=1)
-                nc.vector.scalar_tensor_tensor(
-                    out=junk[:],
-                    in0=w2[jt][:, 0:1024],
-                    scalar=1.0,
-                    in1=w2[jt][:, 1024:2048],
-                    op0=ALU.mult,
-                    op1=ALU.add,
-                    accum_out=pa[:],
-                )
-                nc.vector.tensor_scalar(
-                    out=w2[jt][:, 2048:4096],
-                    in0=w2[jt][:, 2048:4096],
-                    scalar1=float(NH),
-                    scalar2=None,
-                    op0=ALU.mult,
-                    op1=ALU.add,
-                    accum_out=pb[:],
-                )
-                nc.vector.scalar_tensor_tensor(
-                    out=c_col[:], in0=pa[:], scalar=float(NH), in1=pb[:], op0=ALU.mult, op1=ALU.add
-                )
-            else:
-                nc.vector.tensor_scalar(
-                    out=w2[jt][:],
-                    in0=w2[jt][:],
-                    scalar1=float(NH),
-                    scalar2=None,
-                    op0=ALU.mult,
-                    op1=ALU.add,
-                    accum_out=c_col[:],
-                )
+        def product(jt):
             mm = ps_a.tile([P, B], F32, name="mm", tag="a")
             for g in range(PASSES):
                 jc = slice(N * g + P * jt, N * g + P * (jt + 1))
@@ -211,17 +197,123 @@ def tile_advresnet_kernel(tc, x, y, beta, bias_lin, W1, W2, bias1, bias2, adv, o
                     start=(g == 0),
                     stop=(g == PASSES - 1),
                 )
+            held["mm", jt] = mm
+
+        def sum_vector(piece, acc):
+            nc.vector.tensor_scalar(
+                out=piece, in0=piece, scalar1=float(NH), scalar2=None, op0=ALU.mult, op1=ALU.add, accum_out=acc
+            )
+
+        def sum_scalar(piece, acc):
+            nc.scalar.activation(out=piece, in_=piece, func=ACT.Copy, scale=float(NH), accum_out=acc)
+
+        def join(jt):
+            nc.vector.tensor_tensor(out=c_col[jt][:], in0=part_a[jt][:], in1=part_b[jt][:], op=ALU.add)
+
+        def combine(jt):
             o_t = work.tile([P, B], F32, name="o_t", tag="o_t", bufs=3)
             nc.vector.scalar_tensor_tensor(
-                out=o_t[:], in0=mm[:], scalar=c_col[:, 0:1], in1=t_all[:, jt, :], op0=ALU.add, op1=ALU.add
+                out=o_t[:],
+                in0=held["mm", jt][:],
+                scalar=c_col[jt][:, 0:1],
+                in1=held["t_all"][:, jt, :],
+                op0=ALU.add,
+                op1=ALU.add,
             )
             o_ps = ps_b.tile([P, BT, P], F32, name="o_ps", tag="b")
             for t in range(BT):
                 nc.tensor.transpose(out=o_ps[:, t, :], in_=o_t[:, P * t : P * (t + 1)], identity=ident_f[:])
-            nc.scalar.copy(out=out_sb[:, :, P * jt : P * (jt + 1)], in_=o_ps[:])
-            if jt >= 6:
-                sc = slice(P * jt, P * (jt + 1))
-                nc.sync.dma_start(out=out_v[:, :, sc], in_=out_sb[:, :, sc])
-            elif jt % 2 == 1:
-                sc = slice(P * (jt - 1), P * (jt + 1))
-                nc.sync.dma_start(out=out_v[:, :, sc], in_=out_sb[:, :, sc])
+            held["o_ps", jt] = o_ps
+
+        def leave(jt):
+            nc.scalar.copy(out=held["out_sb"][:, :, P * jt : P * (jt + 1)], in_=held["o_ps", jt][:])
+
+        def store(j0, j1):
+            sc = slice(P * j0, P * j1)
+            nc.sync.dma_start(out=out_v[:, :, sc], in_=held["out_sb"][:, :, sc])
+
+        lo, hi = slice(0, 2048), slice(2048, 4096)
+
+        beta_copy(0, 0, True)
+        beta_copy(0, 1, False)
+        beta_abs(0)
+        beta_quant(0, 0)
+        bias_cols()
+        beta_norm(0)
+        beta_abs(1)
+        beta_copy(1, 0, True)
+        beta_copy(1, 1, False)
+        beta_quant(0, 1)
+        beta_quant(1, 0)
+        beta_norm(1)
+        beta_abs(2)
+        beta_norm(2)
+        beta_abs(3)
+        beta_norm(3)
+        beta_copy(2, 0, True)
+        beta_copy(2, 1, False)
+        beta_quant(1, 1)
+        beta_quant(2, 0)
+        beta_copy(3, 1, False)
+        beta_copy(3, 0, True)
+        beta_quant(2, 1)
+        norm_cols()
+        for i in range(8):
+            x_turn(i)
+        beta_quant(3, 1)
+        beta_quant(3, 0)
+        for i in range(8):
+            x_quant(i)
+        held["t_all"] = big.tile([P, JT, B], F32, name="t_all", tag="raw_tt")
+        y_turn(0)
+        y_turn(1)
+        for jt in range(4):
+            y_term(jt)
+        y_turn(2)
+        product(0)
+        y_turn(3)
+        for jt in range(4, 8):
+            y_term(jt)
+        product(1)
+        product(2)
+        held["out_sb"] = big.tile([P, BT, N], F32, name="out_sb", tag="x_out")
+        sum_vector(w2[0][:], c_col[0][:])
+        sum_vector(w2[1][:], c_col[1][:])
+        sum_scalar(w2[3][:, lo], part_a[3][:])
+        sum_scalar(w2[3][:, hi], part_b[3][:])
+        combine(0)
+        product(3)
+        leave(0)
+        combine(1)
+        product(4)
+        leave(1)
+        store(0, 2)
+        sum_vector(w2[2][:], c_col[2][:])
+        sum_scalar(w2[6][:, lo], part_a[6][:])
+        combine(2)
+        product(5)
+        join(3)
+        combine(3)
+        product(6)
+        leave(2)
+        leave(3)
+        store(2, 4)
+        sum_scalar(w2[6][:, hi], part_b[6][:])
+        sum_vector(w2[4][:], c_col[4][:])
+        combine(4)
+        product(7)
+        sum_vector(w2[5][:], c_col[5][:])
+        leave(4)
+        sum_scalar(w2[7][:, lo], part_a[7][:])
+        combine(5)
+        join(6)
+        combine(6)
+        leave(5)
+        store(4, 6)
+        leave(6)
+        store(6, 7)
+        sum_vector(w2[7][:, hi], part_b[7][:])
+        join(7)
+        combine(7)
+        leave(7)
+        store(7, 8)

@@ -304,7 +304,6 @@ def tile_advresnet_kernel(tc, x, y, beta, bias_lin, W1, W2, bias1, bias2, adv, o
         product(7)
         sum_vector(w2[5][:], c_col[5][:])
         leave(4)
-        sum_scalar(w2[7][:, lo], part_a[7][:])
         combine(5)
         join(6)
         combine(6)
@@ -312,6 +311,7 @@ def tile_advresnet_kernel(tc, x, y, beta, bias_lin, W1, W2, bias1, bias2, adv, o
         store(4, 6)
         leave(6)
         store(6, 7)
+        sum_vector(w2[7][:, lo], part_a[7][:])
         sum_vector(w2[7][:, hi], part_b[7][:])
         join(7)
         combine(7)

@@ -15,15 +15,20 @@ ACT = mybir.ActivationFunctionType
 P = 128
 B, K, NH, N = 512, 2048, 4096, 1024
 EPSILON = 0.1
-PASSES = K // 512
+K_PASS = 4 * P
+PASSES = K // K_PASS
+PASS_ELEMS = 4 * N
+HALF = N // 2
 JT = N // P
 BT = B // P
+W2_HALF = NH // 2
 ONES_N = 32
 
 FLOPS = 2 * B * K * N
 BYTES = 2 * (B * K + B * N + K * N + N * NH + 2 * N) + 4 * B * N
 
-LOAD_ORDER = (0, 1, 3, 2, 6, 4, 5)
+W2_LOAD_ORDER = (0, 1, 3, 2, 6, 4, 5)
+SPLIT_TILES = (3, 6, 7)
 
 
 def tile_advresnet_kernel(tc, x, y, beta, bias_lin, W1, W2, bias1, bias2, adv, out):
@@ -40,8 +45,8 @@ def tile_advresnet_kernel(tc, x, y, beta, bias_lin, W1, W2, bias1, bias2, adv, o
 
         brows = const.tile([P, P], BF16, name="brows")
         nc.gpsimd.memset(brows[:], 0.0)
-        nc.scalar.dma_start(out=brows[0:8, :], in_=bias_lin.rearrange("(r c) -> r c", c=P))
-        nc.scalar.dma_start(out=brows[8:16, :], in_=bias2.rearrange("(r c) -> r c", c=P))
+        nc.scalar.dma_start(out=brows[0:JT, :], in_=bias_lin.rearrange("(r c) -> r c", c=P))
+        nc.scalar.dma_start(out=brows[JT : 2 * JT, :], in_=bias2.rearrange("(r c) -> r c", c=P))
         ident_b = const.tile([P, P], BF16, name="ident_b")
         make_identity(nc, ident_b[:])
         ident_f = const.tile([P, P], F32, name="ident_f")
@@ -49,222 +54,228 @@ def tile_advresnet_kernel(tc, x, y, beta, bias_lin, W1, W2, bias1, bias2, adv, o
         ones = const.tile([P, ONES_N], BF16, name="ones")
         nc.vector.memset(ones[:], 1.0)
 
-        raw = big.tile([P, PASSES * 4096], BF16, name="raw", tag="raw_tt")
+        raw = big.tile([P, PASSES * PASS_ELEMS], BF16, name="raw", tag="raw_tt")
         raw_planes = raw[:].rearrange("q (g t w) -> q g t w", g=PASSES, t=4)
         for h in range(2):
             for u in range(2):
                 nc.sync.dma_start(
-                    out=raw_planes[:, 0, 2 * u : 2 * u + 2, 512 * h : 512 * (h + 1)],
-                    in_=beta[256 * u : 256 * (u + 1), 512 * h : 512 * (h + 1)].rearrange("(q e) w -> q e w", e=2),
+                    out=raw_planes[:, 0, 2 * u : 2 * u + 2, HALF * h : HALF * (h + 1)],
+                    in_=beta[256 * u : 256 * (u + 1), HALF * h : HALF * (h + 1)].rearrange("(q e) w -> q e w", e=2),
                 )
         for g in range(1, PASSES):
             nc.sync.dma_start(
-                out=raw[:, 4096 * g : 4096 * (g + 1)].rearrange("q (u r) -> q u r", u=2),
-                in_=beta[512 * g : 512 * (g + 1), :].rearrange("(u q e) w -> q u (e w)", u=2, e=2),
+                out=raw[:, PASS_ELEMS * g : PASS_ELEMS * (g + 1)].rearrange("q (u r) -> q u r", u=2),
+                in_=beta[K_PASS * g : K_PASS * (g + 1), :].rearrange("(u q e) w -> q u (e w)", u=2, e=2),
             )
         x_sb = big.tile([P, BT * K], BF16, name="x_sb", tag="x_out")
         x_rows = x.rearrange("(p t) k -> p (t k)", t=BT)
         for h in range(2):
-            nc.sync.dma_start(out=x_sb[:, 4096 * h : 4096 * (h + 1)], in_=x_rows[:, 4096 * h : 4096 * (h + 1)])
+            nc.sync.dma_start(out=x_sb[:, 2 * K * h : 2 * K * (h + 1)], in_=x_rows[:, 2 * K * h : 2 * K * (h + 1)])
         y_sb = big.tile([P, BT * N], BF16, name="y_sb")
         nc.sync.dma_start(out=y_sb[:], in_=y.rearrange("(p t) j -> p (t j)", t=BT))
         w2 = [big.tile([P, NH], BF16, name="w2_%d" % jt) for jt in range(JT)]
-        for jt in LOAD_ORDER:
+        for jt in W2_LOAD_ORDER:
             nc.sync.dma_start(out=w2[jt][:], in_=W2[P * jt : P * (jt + 1), :])
         for i in range(2):
             nc.sync.dma_start(
-                out=w2[JT - 1][:, 2048 * i : 2048 * (i + 1)],
-                in_=W2[P * (JT - 1) : P * JT, 2048 * i : 2048 * (i + 1)],
+                out=w2[JT - 1][:, W2_HALF * i : W2_HALF * (i + 1)],
+                in_=W2[P * (JT - 1) : P * JT, W2_HALF * i : W2_HALF * (i + 1)],
             )
 
         codes_b = big.tile([P, PASSES * N], U32, name="codes_b", align_bytes=64)
-        plane_b = big.tile([P, PASSES * N], U8, name="plane_b", align_bytes=64)
+        scales_b = big.tile([P, PASSES * N], U8, name="plane_b", align_bytes=64)
         codes_x = big.tile([P, PASSES * B], U32, name="codes_x", align_bytes=64)
-        plane_x = big.tile([P, PASSES * B], U8, name="plane_x", align_bytes=64)
-        b16 = const.tile([P, 16], F32, name="b16")
+        scales_x = big.tile([P, PASSES * B], U8, name="plane_x", align_bytes=64)
+        b16 = const.tile([P, 2 * JT], F32, name="b16")
         bsum = const.tile([P, JT], F32, name="bsum")
-        sraw = const.tile([P, JT], F32, name="sraw")
-        s_col = const.tile([P, JT], F32, name="s_col")
-        c_col = [const.tile([P, 1], F32, name="c_%d" % jt) for jt in range(JT)]
-        part_a = [const.tile([P, 1], F32, name="pa_%d" % jt) for jt in range(JT)]
-        part_b = [const.tile([P, 1], F32, name="pb_%d" % jt) for jt in range(JT)]
-        xw = x_sb[:].bitcast(F32)
-        out_v = out.rearrange("(p t) j -> p t j", t=BT)
+        norm = const.tile([P, JT], F32, name="sraw")
+        y_scale = const.tile([P, JT], F32, name="s_col")
+        w2_sum = [const.tile([P, 1], F32, name="c_%d" % jt) for jt in range(JT)]
+        half_a = dict((jt, const.tile([P, 1], F32, name="pa_%d" % jt)) for jt in SPLIT_TILES)
+        half_b = dict((jt, const.tile([P, 1], F32, name="pb_%d" % jt)) for jt in SPLIT_TILES)
+        x_words = x_sb[:].bitcast(F32)
+        out_rows = out.rearrange("(p t) j -> p t j", t=BT)
         held = {}
 
-        bt_ps = ps_c.tile([P, P], BF16, name="bt_ps", tag="c")
-        nc.tensor.transpose(out=bt_ps[:], in_=brows[:], identity=ident_b[:])
-        bn = [ps_b.tile([P, 4, PASSES, ONES_N], F32, name="bn_%d" % i, tag="b") for i in range(2)]
+        bias_t = ps_c.tile([P, P], BF16, name="bt_ps", tag="c")
+        nc.tensor.transpose(out=bias_t[:], in_=brows[:], identity=ident_b[:])
+        norm_ps = [ps_b.tile([P, JT // 2, PASSES, ONES_N], F32, name="bn_%d" % i, tag="b") for i in range(2)]
 
-        def bias_cols():
-            nc.vector.tensor_copy(out=b16[:], in_=bt_ps[:, 0:16])
-            nc.vector.tensor_tensor(out=bsum[:], in0=b16[:, 0:8], in1=b16[:, 8:16], op=ALU.add)
+        def bias_columns():
+            nc.vector.tensor_copy(out=b16[:], in_=bias_t[:, 0 : 2 * JT])
+            nc.vector.tensor_tensor(out=bsum[:], in0=b16[:, 0:JT], in1=b16[:, JT : 2 * JT], op=ALU.add)
 
         def beta_abs(g):
-            ab = work.tile([P, 2048], I32, name="ab", tag="ab")
+            ab = work.tile([P, PASS_ELEMS // 2], I32, name="ab", tag="ab")
             nc.vector.tensor_single_scalar(
-                out=ab[:], in_=raw[:, 4096 * g : 4096 * (g + 1)].bitcast(I32), scalar=0x7FFF7FFF, op=ALU.bitwise_and
+                out=ab[:],
+                in_=raw[:, PASS_ELEMS * g : PASS_ELEMS * (g + 1)].bitcast(I32),
+                scalar=0x7FFF7FFF,
+                op=ALU.bitwise_and,
             )
             held["ab", g] = ab
 
-        def beta_copy(g, h, on_vector):
-            gb = work.tile([P, 2048], BF16, name="gb", tag="gb", bufs=8, align_bytes=64)
-            src = raw_planes[:, g, :, 512 * h : 512 * (h + 1)].rearrange("q t (c i) -> q c t i", i=4)
-            dst = gb[:].rearrange("q (c i t) -> q c t i", i=4, t=4)
+        def beta_regroup(g, h, on_vector):
+            grouped = work.tile([P, 4 * HALF], BF16, name="gb", tag="gb", bufs=2 * PASSES, align_bytes=64)
+            src = raw_planes[:, g, :, HALF * h : HALF * (h + 1)].rearrange("q t (c i) -> q c t i", i=4)
+            dst = grouped[:].rearrange("q (c i t) -> q c t i", i=4, t=4)
             if on_vector:
                 nc.vector.tensor_copy(out=dst, in_=src)
             else:
                 nc.scalar.copy(out=dst, in_=src)
-            held["gb", g, h] = gb
+            held["gb", g, h] = grouped
 
-        def beta_quant(g, h):
-            cols = slice(N * g + 512 * h, N * g + 512 * (h + 1))
+        def beta_quantise(g, h):
+            cols = slice(N * g + HALF * h, N * g + HALF * (h + 1))
             nc.vector.quantize_mx(
-                out=codes_b[:, cols].bitcast(FP8X4), scales=plane_b[:, cols], in_=held["gb", g, h][:]
+                out=codes_b[:, cols].bitcast(FP8X4), scales=scales_b[:, cols], in_=held["gb", g, h][:]
             )
 
-        def beta_norm(g):
-            abv = held["ab", g][:].bitcast(BF16)
+        def beta_norm_pass(g):
+            planes = held["ab", g][:].bitcast(BF16)
             for jt in range(JT):
                 for t in range(4):
                     nc.tensor.matmul(
-                        out=bn[jt // 4][:, jt % 4, g, :],
-                        lhsT=abv[:, N * t + P * jt : N * t + P * (jt + 1)],
+                        out=norm_ps[jt // 4][:, jt % 4, g, :],
+                        lhsT=planes[:, N * t + P * jt : N * t + P * (jt + 1)],
                         rhs=ones[:],
                         start=(t == 0),
                         stop=(t == 3),
                     )
 
-        def norm_cols():
+        def norm_columns():
             for i in range(2):
                 nc.vector.tensor_reduce(
-                    out=sraw[:, 4 * i : 4 * (i + 1)], in_=bn[i][:, :, :, 0], axis=mybir.AxisListType.X, op=ALU.add
+                    out=norm[:, 4 * i : 4 * (i + 1)], in_=norm_ps[i][:, :, :, 0], axis=mybir.AxisListType.X, op=ALU.add
                 )
-            nc.vector.tensor_scalar_mul(out=s_col[:], in0=sraw[:], scalar1=-EPSILON)
+            nc.vector.tensor_scalar_mul(out=y_scale[:], in0=norm[:], scalar1=-EPSILON)
 
         def x_turn(i):
             h, g = i // PASSES, i % PASSES
-            xt = ps_a.tile([P, 2, 256], F32, name="xt", tag="a")
+            turned = ps_a.tile([P, 2, 2 * P], F32, name="xt", tag="a")
             for u in range(2):
-                for tt in range(2):
-                    w0 = 1024 * (2 * h + tt) + 256 * g + 128 * u
+                for s in range(2):
+                    w0 = (K // 2) * (2 * h + s) + 256 * g + P * u
                     nc.tensor.transpose(
-                        out=xt[:, u, P * tt : P * (tt + 1)], in_=xw[:, w0 : w0 + P], identity=ident_f[:]
+                        out=turned[:, u, P * s : P * (s + 1)], in_=x_words[:, w0 : w0 + P], identity=ident_f[:]
                     )
-            gx = work.tile([P, 1024], BF16, name="gx", tag="gx", bufs=8, align_bytes=64)
+            grouped = work.tile([P, 8 * P], BF16, name="gx", tag="gx", bufs=2 * PASSES, align_bytes=64)
             nc.scalar.copy(
-                out=gx[:].bitcast(F32).rearrange("q (c u) -> q c u", u=2), in_=xt[:].rearrange("q u c -> q c u")
+                out=grouped[:].bitcast(F32).rearrange("q (c u) -> q c u", u=2),
+                in_=turned[:].rearrange("q u c -> q c u"),
             )
-            held["gx", i] = gx
+            held["gx", i] = grouped
 
-        def x_quant(i):
+        def x_quantise(i):
             h, g = i // PASSES, i % PASSES
-            cols = slice(B * g + 256 * h, B * g + 256 * (h + 1))
-            nc.vector.quantize_mx(out=codes_x[:, cols].bitcast(FP8X4), scales=plane_x[:, cols], in_=held["gx", i][:])
+            cols = slice(B * g + 2 * P * h, B * g + 2 * P * (h + 1))
+            nc.vector.quantize_mx(out=codes_x[:, cols].bitcast(FP8X4), scales=scales_x[:, cols], in_=held["gx", i][:])
 
         def y_turn(m):
-            y_t = ps_c.tile([P, 2, B], BF16, name="y_t", tag="c")
+            turned = ps_c.tile([P, 2, B], BF16, name="y_t", tag="c")
             for i in range(2):
                 jt = 2 * m + i
                 for t in range(BT):
                     nc.tensor.transpose(
-                        out=y_t[:, i, P * t : P * (t + 1)],
+                        out=turned[:, i, P * t : P * (t + 1)],
                         in_=y_sb[:, N * t + P * jt : N * t + P * (jt + 1)],
                         identity=ident_b[:],
                     )
-            held["y_t", m] = y_t
+            held["y_t", m] = turned
 
         def y_term(jt):
             nc.scalar.activation(
-                out=held["t_all"][:, jt, :],
+                out=held["y_terms"][:, jt, :],
                 in_=held["y_t", jt // 2][:, jt % 2, :],
                 func=ACT.Identity,
-                scale=s_col[:, jt : jt + 1],
+                scale=y_scale[:, jt : jt + 1],
                 bias=bsum[:, jt : jt + 1],
             )
 
         def product(jt):
-            mm = ps_a.tile([P, B], F32, name="mm", tag="a")
+            acc = ps_a.tile([P, B], F32, name="mm", tag="a")
             for g in range(PASSES):
-                jc = slice(N * g + P * jt, N * g + P * (jt + 1))
-                bc = slice(B * g, B * (g + 1))
+                j_cols = slice(N * g + P * jt, N * g + P * (jt + 1))
+                b_cols = slice(B * g, B * (g + 1))
                 nc.tensor.matmul_mx(
-                    out=mm[:],
-                    lhsT=codes_b[:, jc].bitcast(FP8X4),
-                    lhsT_scale=plane_b[:, jc],
-                    rhs=codes_x[:, bc].bitcast(FP8X4),
-                    rhs_scale=plane_x[:, bc],
+                    out=acc[:],
+                    lhsT=codes_b[:, j_cols].bitcast(FP8X4),
+                    lhsT_scale=scales_b[:, j_cols],
+                    rhs=codes_x[:, b_cols].bitcast(FP8X4),
+                    rhs_scale=scales_x[:, b_cols],
                     start=(g == 0),
                     stop=(g == PASSES - 1),
                 )
-            held["mm", jt] = mm
+            held["mm", jt] = acc
 
-        def sum_vector(piece, acc):
+        def sum_on_vector(piece, total):
             nc.vector.tensor_scalar(
-                out=piece, in0=piece, scalar1=float(NH), scalar2=None, op0=ALU.mult, op1=ALU.add, accum_out=acc
+                out=piece, in0=piece, scalar1=float(NH), scalar2=None, op0=ALU.mult, op1=ALU.add, accum_out=total
             )
 
-        def sum_scalar(piece, acc):
-            nc.scalar.activation(out=piece, in_=piece, func=ACT.Copy, scale=float(NH), accum_out=acc)
+        def sum_on_scalar(piece, total):
+            nc.scalar.activation(out=piece, in_=piece, func=ACT.Copy, scale=float(NH), accum_out=total)
 
-        def join(jt):
-            nc.vector.tensor_tensor(out=c_col[jt][:], in0=part_a[jt][:], in1=part_b[jt][:], op=ALU.add)
+        def join_halves(jt):
+            nc.vector.tensor_tensor(out=w2_sum[jt][:], in0=half_a[jt][:], in1=half_b[jt][:], op=ALU.add)
 
         def combine(jt):
-            o_t = work.tile([P, B], F32, name="o_t", tag="o_t", bufs=3)
+            tile_t = work.tile([P, B], F32, name="o_t", tag="o_t", bufs=3)
             nc.vector.scalar_tensor_tensor(
-                out=o_t[:],
+                out=tile_t[:],
                 in0=held["mm", jt][:],
-                scalar=c_col[jt][:, 0:1],
-                in1=held["t_all"][:, jt, :],
+                scalar=w2_sum[jt][:, 0:1],
+                in1=held["y_terms"][:, jt, :],
                 op0=ALU.add,
                 op1=ALU.add,
             )
-            o_ps = ps_b.tile([P, BT, P], F32, name="o_ps", tag="b")
+            turned = ps_b.tile([P, BT, P], F32, name="o_ps", tag="b")
             for t in range(BT):
-                nc.tensor.transpose(out=o_ps[:, t, :], in_=o_t[:, P * t : P * (t + 1)], identity=ident_f[:])
-            held["o_ps", jt] = o_ps
+                nc.tensor.transpose(out=turned[:, t, :], in_=tile_t[:, P * t : P * (t + 1)], identity=ident_f[:])
+            held["o_ps", jt] = turned
 
-        def leave(jt):
+        def leave_psum(jt):
             nc.scalar.copy(out=held["out_sb"][:, :, P * jt : P * (jt + 1)], in_=held["o_ps", jt][:])
 
-        def store(j0, j1):
-            sc = slice(P * j0, P * j1)
-            nc.sync.dma_start(out=out_v[:, :, sc], in_=held["out_sb"][:, :, sc])
+        def store(first, end):
+            cols = slice(P * first, P * end)
+            nc.sync.dma_start(out=out_rows[:, :, cols], in_=held["out_sb"][:, :, cols])
 
-        lo, hi = slice(0, 2048), slice(2048, 4096)
+        left, right = slice(0, W2_HALF), slice(W2_HALF, NH)
 
-        beta_copy(0, 0, True)
-        beta_copy(0, 1, False)
+        beta_regroup(0, 0, True)
+        beta_regroup(0, 1, False)
         beta_abs(0)
-        beta_quant(0, 0)
-        bias_cols()
-        beta_norm(0)
+        beta_quantise(0, 0)
+        bias_columns()
+        beta_norm_pass(0)
         beta_abs(1)
-        beta_copy(1, 0, True)
-        beta_copy(1, 1, False)
-        beta_quant(0, 1)
-        beta_quant(1, 0)
-        beta_norm(1)
+        beta_regroup(1, 0, True)
+        beta_regroup(1, 1, False)
+        beta_quantise(0, 1)
+        beta_quantise(1, 0)
+        beta_norm_pass(1)
         beta_abs(2)
-        beta_norm(2)
+        beta_norm_pass(2)
         beta_abs(3)
-        beta_norm(3)
-        beta_copy(2, 0, True)
-        beta_copy(2, 1, False)
-        beta_quant(1, 1)
-        beta_quant(2, 0)
-        beta_copy(3, 1, False)
-        beta_copy(3, 0, True)
-        beta_quant(2, 1)
-        norm_cols()
-        for i in range(8):
+        beta_norm_pass(3)
+        beta_regroup(2, 0, True)
+        beta_regroup(2, 1, False)
+        beta_quantise(1, 1)
+        beta_quantise(2, 0)
+        beta_regroup(3, 1, False)
+        beta_regroup(3, 0, True)
+        beta_quantise(2, 1)
+        norm_columns()
+
+        for i in range(2 * PASSES):
             x_turn(i)
-        beta_quant(3, 1)
-        beta_quant(3, 0)
-        for i in range(8):
-            x_quant(i)
-        held["t_all"] = big.tile([P, JT, B], F32, name="t_all", tag="raw_tt")
+        beta_quantise(3, 1)
+        beta_quantise(3, 0)
+        for i in range(2 * PASSES):
+            x_quantise(i)
+
+        held["y_terms"] = big.tile([P, JT, B], F32, name="t_all", tag="raw_tt")
         y_turn(0)
         y_turn(1)
         for jt in range(4):
@@ -272,48 +283,49 @@ def tile_advresnet_kernel(tc, x, y, beta, bias_lin, W1, W2, bias1, bias2, adv, o
         y_turn(2)
         product(0)
         y_turn(3)
-        for jt in range(4, 8):
+        for jt in range(4, JT):
             y_term(jt)
         product(1)
         product(2)
+
         held["out_sb"] = big.tile([P, BT, N], F32, name="out_sb", tag="x_out")
-        sum_vector(w2[0][:], c_col[0][:])
-        sum_vector(w2[1][:], c_col[1][:])
-        sum_scalar(w2[3][:, lo], part_a[3][:])
-        sum_scalar(w2[3][:, hi], part_b[3][:])
+        sum_on_vector(w2[0][:], w2_sum[0][:])
+        sum_on_vector(w2[1][:], w2_sum[1][:])
+        sum_on_scalar(w2[3][:, left], half_a[3][:])
+        sum_on_scalar(w2[3][:, right], half_b[3][:])
         combine(0)
         product(3)
-        leave(0)
+        leave_psum(0)
         combine(1)
         product(4)
-        leave(1)
+        leave_psum(1)
         store(0, 2)
-        sum_vector(w2[2][:], c_col[2][:])
-        sum_scalar(w2[6][:, lo], part_a[6][:])
+        sum_on_vector(w2[2][:], w2_sum[2][:])
+        sum_on_scalar(w2[6][:, left], half_a[6][:])
         combine(2)
         product(5)
-        join(3)
+        join_halves(3)
         combine(3)
         product(6)
-        leave(2)
-        leave(3)
+        leave_psum(2)
+        leave_psum(3)
         store(2, 4)
-        sum_scalar(w2[6][:, hi], part_b[6][:])
-        sum_vector(w2[4][:], c_col[4][:])
+        sum_on_scalar(w2[6][:, right], half_b[6][:])
+        sum_on_vector(w2[4][:], w2_sum[4][:])
         combine(4)
         product(7)
-        sum_vector(w2[5][:], c_col[5][:])
-        leave(4)
+        sum_on_vector(w2[5][:], w2_sum[5][:])
+        leave_psum(4)
+        sum_on_scalar(w2[7][:, left], half_a[7][:])
         combine(5)
-        join(6)
+        join_halves(6)
         combine(6)
-        leave(5)
+        leave_psum(5)
         store(4, 6)
-        leave(6)
+        leave_psum(6)
         store(6, 7)
-        sum_vector(w2[7][:, lo], part_a[7][:])
-        sum_vector(w2[7][:, hi], part_b[7][:])
-        join(7)
+        sum_on_vector(w2[7][:, right], half_b[7][:])
+        join_halves(7)
         combine(7)
-        leave(7)
+        leave_psum(7)
         store(7, 8)

from contextlib import ExitStack

import concourse.mybir as mybir
from concourse.masks import make_identity

F32 = mybir.dt.float32
BF16 = mybir.dt.bfloat16
I32 = mybir.dt.int32
U32 = mybir.dt.uint32
U8 = mybir.dt.uint8
FP8X4 = mybir.dt.float8_e4m3fn_x4
ALU = mybir.AluOpType
ACT = mybir.ActivationFunctionType

P = 128
B, K, NH, N = 512, 2048, 4096, 1024
EPSILON = 0.1
K_PASS = 4 * P
PASSES = K // K_PASS
PASS_ELEMS = 4 * N
HALF = N // 2
JT = N // P
BT = B // P
W2_HALF = NH // 2
ONES_N = 32

FLOPS = 2 * B * K * N
BYTES = 2 * (B * K + B * N + K * N + N * NH + 2 * N) + 4 * B * N

W2_LOAD_ORDER = (0, 1, 3, 2, 6, 4, 5)
SPLIT_TILES = (3, 6, 7)


def tile_advresnet_kernel(tc, x, y, beta, bias_lin, W1, W2, bias1, bias2, adv, out):
    assert adv == 1
    nc = tc.nc
    with ExitStack() as ctx:
        const = ctx.enter_context(tc.tile_pool(name="const", bufs=1))
        big = ctx.enter_context(tc.tile_pool(name="big", bufs=1))
        work = ctx.enter_context(tc.tile_pool(name="work", bufs=2))
        ps_a = ctx.enter_context(tc.psum_pool(name="ps_a", bufs=3))
        ps_b = ctx.enter_context(tc.psum_pool(name="ps_b", bufs=3))
        ps_c = ctx.enter_context(tc.psum_pool(name="ps_c", bufs=2))
        ctx.enter_context(tc.manual_schedule())

        brows = const.tile([P, P], BF16, name="brows")
        nc.gpsimd.memset(brows[:], 0.0)
        nc.scalar.dma_start(out=brows[0:JT, :], in_=bias_lin.rearrange("(r c) -> r c", c=P))
        nc.scalar.dma_start(out=brows[JT : 2 * JT, :], in_=bias2.rearrange("(r c) -> r c", c=P))
        ident_b = const.tile([P, P], BF16, name="ident_b")
        make_identity(nc, ident_b[:])
        ident_f = const.tile([P, P], F32, name="ident_f")
        make_identity(nc, ident_f[:])
        ones = const.tile([P, ONES_N], BF16, name="ones")
        nc.vector.memset(ones[:], 1.0)

        raw = big.tile([P, PASSES * PASS_ELEMS], BF16, name="raw", tag="raw_tt")
        raw_planes = raw[:].rearrange("q (g t w) -> q g t w", g=PASSES, t=4)
        for h in range(2):
            for u in range(2):
                nc.sync.dma_start(
                    out=raw_planes[:, 0, 2 * u : 2 * u + 2, HALF * h : HALF * (h + 1)],
                    in_=beta[256 * u : 256 * (u + 1), HALF * h : HALF * (h + 1)].rearrange("(q e) w -> q e w", e=2),
                )
        for g in range(1, PASSES):
            nc.sync.dma_start(
                out=raw[:, PASS_ELEMS * g : PASS_ELEMS * (g + 1)].rearrange("q (u r) -> q u r", u=2),
                in_=beta[K_PASS * g : K_PASS * (g + 1), :].rearrange("(u q e) w -> q u (e w)", u=2, e=2),
            )
        x_sb = big.tile([P, BT * K], BF16, name="x_sb", tag="x_out")
        x_rows = x.rearrange("(p t) k -> p (t k)", t=BT)
        for h in range(2):
            nc.sync.dma_start(out=x_sb[:, 2 * K * h : 2 * K * (h + 1)], in_=x_rows[:, 2 * K * h : 2 * K * (h + 1)])
        y_sb = big.tile([P, BT * N], BF16, name="y_sb")
        nc.sync.dma_start(out=y_sb[:], in_=y.rearrange("(p t) j -> p (t j)", t=BT))
        w2 = [big.tile([P, NH], BF16, name="w2_%d" % jt) for jt in range(JT)]
        for jt in W2_LOAD_ORDER:
            nc.sync.dma_start(out=w2[jt][:], in_=W2[P * jt : P * (jt + 1), :])
        for i in range(2):
            nc.sync.dma_start(
                out=w2[JT - 1][:, W2_HALF * i : W2_HALF * (i + 1)],
                in_=W2[P * (JT - 1) : P * JT, W2_HALF * i : W2_HALF * (i + 1)],
            )

        codes_b = big.tile([P, PASSES * N], U32, name="codes_b", align_bytes=64)
        scales_b = big.tile([P, PASSES * N], U8, name="plane_b", align_bytes=64)
        codes_x = big.tile([P, PASSES * B], U32, name="codes_x", align_bytes=64)
        scales_x = big.tile([P, PASSES * B], U8, name="plane_x", align_bytes=64)
        b16 = const.tile([P, 2 * JT], F32, name="b16")
        bsum = const.tile([P, JT], F32, name="bsum")
        norm = const.tile([P, JT], F32, name="sraw")
        y_scale = const.tile([P, JT], F32, name="s_col")
        w2_sum = [const.tile([P, 1], F32, name="c_%d" % jt) for jt in range(JT)]
        half_a = dict((jt, const.tile([P, 1], F32, name="pa_%d" % jt)) for jt in SPLIT_TILES)
        half_b = dict((jt, const.tile([P, 1], F32, name="pb_%d" % jt)) for jt in SPLIT_TILES)
        x_words = x_sb[:].bitcast(F32)
        out_rows = out.rearrange("(p t) j -> p t j", t=BT)
        held = {}

        bias_t = ps_c.tile([P, P], BF16, name="bt_ps", tag="c")
        nc.tensor.transpose(out=bias_t[:], in_=brows[:], identity=ident_b[:])
        norm_ps = [ps_b.tile([P, JT // 2, PASSES, ONES_N], F32, name="bn_%d" % i, tag="b") for i in range(2)]

        def bias_columns():
            nc.vector.tensor_copy(out=b16[:], in_=bias_t[:, 0 : 2 * JT])
            nc.vector.tensor_tensor(out=bsum[:], in0=b16[:, 0:JT], in1=b16[:, JT : 2 * JT], op=ALU.add)

        def beta_abs(g):
            ab = work.tile([P, PASS_ELEMS // 2], I32, name="ab", tag="ab")
            nc.vector.tensor_single_scalar(
                out=ab[:],
                in_=raw[:, PASS_ELEMS * g : PASS_ELEMS * (g + 1)].bitcast(I32),
                scalar=0x7FFF7FFF,
                op=ALU.bitwise_and,
            )
            held["ab", g] = ab

        def beta_regroup(g, h, on_vector):
            grouped = work.tile([P, 4 * HALF], BF16, name="gb", tag="gb", bufs=2 * PASSES, align_bytes=64)
            src = raw_planes[:, g, :, HALF * h : HALF * (h + 1)].rearrange("q t (c i) -> q c t i", i=4)
            dst = grouped[:].rearrange("q (c i t) -> q c t i", i=4, t=4)
            if on_vector:
                nc.vector.tensor_copy(out=dst, in_=src)
            else:
                nc.scalar.copy(out=dst, in_=src)
            held["gb", g, h] = grouped

        def beta_quantise(g, h):
            cols = slice(N * g + HALF * h, N * g + HALF * (h + 1))
            nc.vector.quantize_mx(
                out=codes_b[:, cols].bitcast(FP8X4), scales=scales_b[:, cols], in_=held["gb", g, h][:]
            )

        def beta_norm_pass(g):
            planes = held["ab", g][:].bitcast(BF16)
            for jt in range(JT):
                for t in range(4):
                    nc.tensor.matmul(
                        out=norm_ps[jt // 4][:, jt % 4, g, :],
                        lhsT=planes[:, N * t + P * jt : N * t + P * (jt + 1)],
                        rhs=ones[:],
                        start=(t == 0),
                        stop=(t == 3),
                    )

        def norm_columns():
            for i in range(2):
                nc.vector.tensor_reduce(
                    out=norm[:, 4 * i : 4 * (i + 1)], in_=norm_ps[i][:, :, :, 0], axis=mybir.AxisListType.X, op=ALU.add
                )
            nc.vector.tensor_scalar_mul(out=y_scale[:], in0=norm[:], scalar1=-EPSILON)

        def x_turn(i):
            h, g = i // PASSES, i % PASSES
            turned = ps_a.tile([P, 2, 2 * P], F32, name="xt", tag="a")
            for u in range(2):
                for s in range(2):
                    w0 = (K // 2) * (2 * h + s) + 256 * g + P * u
                    nc.tensor.transpose(
                        out=turned[:, u, P * s : P * (s + 1)], in_=x_words[:, w0 : w0 + P], identity=ident_f[:]
                    )
            grouped = work.tile([P, 8 * P], BF16, name="gx", tag="gx", bufs=2 * PASSES, align_bytes=64)
            nc.scalar.copy(
                out=grouped[:].bitcast(F32).rearrange("q (c u) -> q c u", u=2),
                in_=turned[:].rearrange("q u c -> q c u"),
            )
            held["gx", i] = grouped

        def x_quantise(i):
            h, g = i // PASSES, i % PASSES
            cols = slice(B * g + 2 * P * h, B * g + 2 * P * (h + 1))
            nc.vector.quantize_mx(out=codes_x[:, cols].bitcast(FP8X4), scales=scales_x[:, cols], in_=held["gx", i][:])

        def y_turn(m):
            turned = ps_c.tile([P, 2, B], BF16, name="y_t", tag="c")
            for i in range(2):
                jt = 2 * m + i
                for t in range(BT):
                    nc.tensor.transpose(
                        out=turned[:, i, P * t : P * (t + 1)],
                        in_=y_sb[:, N * t + P * jt : N * t + P * (jt + 1)],
                        identity=ident_b[:],
                    )
            held["y_t", m] = turned

        def y_term(jt):
            nc.scalar.activation(
                out=held["y_terms"][:, jt, :],
                in_=held["y_t", jt // 2][:, jt % 2, :],
                func=ACT.Identity,
                scale=y_scale[:, jt : jt + 1],
                bias=bsum[:, jt : jt + 1],
            )

        def product(jt):
            acc = ps_a.tile([P, B], F32, name="mm", tag="a")
            for g in range(PASSES):
                j_cols = slice(N * g + P * jt, N * g + P * (jt + 1))
                b_cols = slice(B * g, B * (g + 1))
                nc.tensor.matmul_mx(
                    out=acc[:],
                    lhsT=codes_b[:, j_cols].bitcast(FP8X4),
                    lhsT_scale=scales_b[:, j_cols],
                    rhs=codes_x[:, b_cols].bitcast(FP8X4),
                    rhs_scale=scales_x[:, b_cols],
                    start=(g == 0),
                    stop=(g == PASSES - 1),
                )
            held["mm", jt] = acc

        def sum_on_vector(piece, total):
            nc.vector.tensor_scalar(
                out=piece, in0=piece, scalar1=float(NH), scalar2=None, op0=ALU.mult, op1=ALU.add, accum_out=total
            )

        def sum_on_scalar(piece, total):
            nc.scalar.activation(out=piece, in_=piece, func=ACT.Copy, scale=float(NH), accum_out=total)

        def join_halves(jt):
            nc.vector.tensor_tensor(out=w2_sum[jt][:], in0=half_a[jt][:], in1=half_b[jt][:], op=ALU.add)

        def combine(jt):
            tile_t = work.tile([P, B], F32, name="o_t", tag="o_t", bufs=3)
            nc.vector.scalar_tensor_tensor(
                out=tile_t[:],
                in0=held["mm", jt][:],
                scalar=w2_sum[jt][:, 0:1],
                in1=held["y_terms"][:, jt, :],
                op0=ALU.add,
                op1=ALU.add,
            )
            turned = ps_b.tile([P, BT, P], F32, name="o_ps", tag="b")
            for t in range(BT):
                nc.tensor.transpose(out=turned[:, t, :], in_=tile_t[:, P * t : P * (t + 1)], identity=ident_f[:])
            held["o_ps", jt] = turned

        def leave_psum(jt):
            nc.scalar.copy(out=held["out_sb"][:, :, P * jt : P * (jt + 1)], in_=held["o_ps", jt][:])

        def store(first, end):
            cols = slice(P * first, P * end)
            nc.sync.dma_start(out=out_rows[:, :, cols], in_=held["out_sb"][:, :, cols])

        left, right = slice(0, W2_HALF), slice(W2_HALF, NH)

        beta_regroup(0, 0, True)
        beta_regroup(0, 1, False)
        beta_abs(0)
        beta_quantise(0, 0)
        bias_columns()
        beta_norm_pass(0)
        beta_abs(1)
        beta_regroup(1, 0, True)
        beta_regroup(1, 1, False)
        beta_quantise(0, 1)
        beta_quantise(1, 0)
        beta_norm_pass(1)
        beta_abs(2)
        beta_norm_pass(2)
        beta_abs(3)
        beta_norm_pass(3)
        beta_regroup(2, 0, True)
        beta_regroup(2, 1, False)
        beta_quantise(1, 1)
        beta_quantise(2, 0)
        beta_regroup(3, 1, False)
        beta_regroup(3, 0, True)
        beta_quantise(2, 1)
        norm_columns()

        for i in range(2 * PASSES):
            x_turn(i)
        beta_quantise(3, 1)
        beta_quantise(3, 0)
        for i in range(2 * PASSES):
            x_quantise(i)

        held["y_terms"] = big.tile([P, JT, B], F32, name="t_all", tag="raw_tt")
        y_turn(0)
        y_turn(1)
        for jt in range(4):
            y_term(jt)
        y_turn(2)
        product(0)
        y_turn(3)
        for jt in range(4, JT):
            y_term(jt)
        product(1)
        product(2)

        held["out_sb"] = big.tile([P, BT, N], F32, name="out_sb", tag="x_out")
        sum_on_vector(w2[0][:], w2_sum[0][:])
        sum_on_vector(w2[1][:], w2_sum[1][:])
        sum_on_scalar(w2[3][:, left], half_a[3][:])
        sum_on_scalar(w2[3][:, right], half_b[3][:])
        combine(0)
        product(3)
        leave_psum(0)
        combine(1)
        product(4)
        leave_psum(1)
        store(0, 2)
        sum_on_vector(w2[2][:], w2_sum[2][:])
        sum_on_scalar(w2[6][:, left], half_a[6][:])
        combine(2)
        product(5)
        join_halves(3)
        combine(3)
        product(6)
        leave_psum(2)
        leave_psum(3)
        store(2, 4)
        sum_on_scalar(w2[6][:, right], half_b[6][:])
        sum_on_vector(w2[4][:], w2_sum[4][:])
        combine(4)
        product(7)
        sum_on_vector(w2[5][:], w2_sum[5][:])
        leave_psum(4)
        sum_on_scalar(w2[7][:, left], half_a[7][:])
        combine(5)
        join_halves(6)
        combine(6)
        leave_psum(5)
        store(4, 6)
        leave_psum(6)
        store(6, 7)
        sum_on_vector(w2[7][:, right], half_b[7][:])
        join_halves(7)
        combine(7)
        leave_psum(7)
        store(7, 8)
